import numpy as np
import ml_dtypes


def mxq(x, axis, fmt="e4m3"):
    dtype, down = {"e4m3": (ml_dtypes.float8_e4m3fn, 7), "e5m2": (ml_dtypes.float8_e5m2, 14)}[fmt]
    v = np.moveaxis(np.asarray(x, np.float32).astype(ml_dtypes.bfloat16).astype(np.float64), axis, -1)
    blocks = v.reshape(v.shape[:-1] + (-1, 32))
    amax = np.abs(blocks).max(-1, keepdims=True)
    byte = np.maximum(np.where(amax > 0, np.frexp(amax)[1] - 1 + 127, 0) - down, 1)
    scale = np.exp2(byte - 127.0)
    codes = (blocks / scale).astype(np.float32).astype(dtype).astype(np.float64)
    return np.moveaxis((codes * scale).reshape(v.shape), -1, axis)


WIDE = False


def mx_kscale(k):
    if not WIDE:
        return np.ones(k)
    levels = np.array([10, -10, 5, -5, 0])
    a = np.random.permutation(np.resize(levels, k // 512 * 4)).reshape(k // 512, 4)
    idx = np.arange(k)
    return np.exp2(a[idx // 512, idx % 128 // 32])


BF16 = ml_dtypes.bfloat16


def bf(x):
    return np.asarray(x, np.float32).astype(BF16)


def f64(x):
    return np.asarray(x).astype(np.float64)


B, C, CQ, H, W, D = 1, 512, 128, 64, 64, 2
HP, WP = H // D, W // D
N = HP * WP


def conv1x1(xq, w, b):
    y = xq @ mxq(f64(w), 1, "e4m3").T
    return y.transpose(0, 2, 1).reshape(B, -1, H, W) + f64(b)[None, :, None, None]


def maxpool(y):
    return y.reshape(B, -1, HP, D, WP, D).max(axis=(3, 5))


def setup_inputs():
    s = mx_kscale(C)
    return {"x": bf(np.random.standard_normal((B, C, H, W)) * s[None, :, None, None]),
            "wq": bf(np.random.standard_normal((CQ, C)) * 0.4 / np.sqrt(C) / s[None, :]),
            "bq": bf(np.random.standard_normal(CQ) * 0.1),
            "wk": bf(np.random.standard_normal((CQ, C)) * 0.4 / np.sqrt(C) / s[None, :]),
            "bk": bf(np.random.standard_normal(CQ) * 0.1),
            "wv": bf(np.random.standard_normal((C, C)) / np.sqrt(C) / s[None, :]),
            "bv": bf(np.random.standard_normal(C) * 0.1)}


def reference(x, wq, bq, wk, bk, wv, bv):
    xq = mxq(f64(x), 1, "e4m3").reshape(B, C, H * W).transpose(0, 2, 1)
    q = maxpool(conv1x1(xq, wq, bq)).reshape(B, -1, N).transpose(0, 2, 1)
    k = maxpool(conv1x1(xq, wk, bk)).reshape(B, -1, N)
    v = maxpool(conv1x1(xq, wv, bv)).reshape(B, C, N)
    return q, k, v

@@ -1,0 +1,224 @@
+from contextlib import ExitStack
+
+import concourse.mybir as mybir
+from concourse.masks import make_identity
+
+F32 = mybir.dt.float32
+BF16 = mybir.dt.bfloat16
+U32 = mybir.dt.uint32
+U8 = mybir.dt.uint8
+FP8X4 = mybir.dt.float8_e4m3fn_x4
+ADD = mybir.AluOpType.add
+MULT = mybir.AluOpType.mult
+MAX = mybir.AluOpType.max
+IDENTITY = mybir.ActivationFunctionType.Identity
+
+P = 128
+PACK = 4
+IMAGE_W = 64
+PIXELS = 64 * IMAGE_W
+UNIT = 8 * IMAGE_W
+CHUNK = 2 * UNIT
+N_CHUNKS = PIXELS // CHUNK
+HALF = CHUNK // 2
+POOLED = CHUNK // 4
+BLOCKS = 6
+PAIR = 2
+ROUNDS_PER_CHUNK = BLOCKS // PAIR
+ROUNDS = N_CHUNKS * ROUNDS_PER_CHUNK
+FIRST_CORNER = (0, 0)
+LATER_CORNERS = ((0, 1), (1, 0), (1, 1))
+
+FLOPS = 2 * BLOCKS * P * PACK * P * PIXELS
+
+
+def tile_selfattentionpatch_pa_kernel(tc, x, wq, bq, wk, bk, wv, bv, out_0, out_1, out_2):
+    nc = tc.nc
+    with ExitStack() as ctx:
+        keep = ctx.enter_context(tc.tile_pool(name="keep", bufs=1))
+        scratch = ctx.enter_context(tc.tile_pool(name="scratch", bufs=8))
+        psum = ctx.enter_context(tc.psum_pool(name="psum", bufs=8))
+        ctx.enter_context(tc.manual_schedule())
+
+        x_rows = x[0].rearrange("(p t) h w -> p t (h w)", t=PACK)
+        q_out = out_0[0].rearrange("(s n) o -> n s o", n=P)
+        k_out = out_1[0]
+        v_out = out_2[0].rearrange("(b o) n -> o b n", o=P)
+
+        ident = keep.tile([P, P], F32)
+        table_warmer = keep.tile([P, 2], F32)
+        bias_rows = keep.tile([P, P], BF16)
+        bias_rows_f32 = keep.tile([P, P], F32)
+        bias = keep.tile([P, BLOCKS], F32)
+        w_rows = keep.tile([P, BLOCKS, PACK * P], BF16)
+        w_grouped = keep.tile([P, BLOCKS, P, PACK], BF16, align_bytes=64)
+        w_codes = keep.tile([P, BLOCKS, P], U32, align_bytes=64)
+        w_scales = keep.tile([P, BLOCKS, P], U8, align_bytes=64)
+        x_raw = [keep.tile([P, PACK, UNIT], BF16, name="x_raw%d" % u) for u in range(PIXELS // UNIT)]
+        x_grouped = [
+            keep.tile([P, 2, HALF, PACK], BF16, name="x_grouped%d" % c, align_bytes=64)
+            for c in range(N_CHUNKS)
+        ]
+        x_codes = [keep.tile([P, 2, HALF], U32, name="x_codes%d" % c, align_bytes=64) for c in range(N_CHUNKS)]
+        x_scales = [keep.tile([P, 2, HALF], U8, name="x_scales%d" % c, align_bytes=64) for c in range(N_CHUNKS)]
+        pooled = [keep.tile([P, BLOCKS, POOLED], F32, name="pooled%d" % c) for c in range(N_CHUNKS)]
+        q_rows = [keep.tile([P, POOLED // P, P], F32, name="q_rows%d" % c) for c in range(N_CHUNKS)]
+        banks = {}
+        running = {}
+
+        def new_bank():
+            return psum.tile([P, HALF], F32, name="bank", tag="bank")
+
+        def load_unit(u):
+            nc.sync.dma_start(out=x_raw[u][:], in_=x_rows[:, :, u * UNIT : (u + 1) * UNIT])
+
+        def regroup_unit(u):
+            c, h = divmod(u, CHUNK // UNIT)
+            by_parity = x_raw[u][:].rearrange("p t (i d w) -> p d i w t", d=2, w=IMAGE_W)
+            columns = slice(h * (UNIT // 2), (h + 1) * (UNIT // 2))
+            even = x_grouped[c][:, 0, columns, :].rearrange("p (i w) t -> p i w t", w=IMAGE_W)
+            odd = x_grouped[c][:, 1, columns, :].rearrange("p (i w) t -> p i w t", w=IMAGE_W)
+            nc.scalar.copy(out=even, in_=by_parity[:, 0])
+            nc.gpsimd.tensor_scalar(out=odd, in0=by_parity[:, 1], scalar1=1.0, scalar2=0.0, op0=MULT, op1=ADD)
+
+        def quantise_chunk(c):
+            for parity in range(2):
+                nc.vector.quantize_mx(
+                    out=x_codes[c][:, parity, :].bitcast(FP8X4),
+                    scales=x_scales[c][:, parity, :],
+                    in_=x_grouped[c][:, parity].rearrange("p n t -> p (n t)"),
+                )
+
+        def prepare_weights(lead):
+            words = w_rows[:].bitcast(F32).rearrange("o b (p u) -> o b u p", u=2)
+            bank = new_bank()
+            for j in range(PAIR):
+                for u in range(2):
+                    nc.tensor.transpose(
+                        bank[:, (2 * j + u) * P : (2 * j + u + 1) * P], words[:, lead + j, u, :], ident[:]
+                    )
+            both = slice(lead, lead + PAIR)
+            nc.scalar.copy(
+                out=w_grouped[:].bitcast(F32)[:, both],
+                in_=bank[:].rearrange("p (j u o) -> p j o u", j=PAIR, u=2),
+            )
+            nc.vector.quantize_mx(
+                out=w_codes[:, both, :].rearrange("p b o -> p (b o)").bitcast(FP8X4),
+                scales=w_scales[:, both, :].rearrange("p b o -> p (b o)"),
+                in_=w_grouped[:, both].rearrange("p b o t -> p (b o t)"),
+            )
+
+        def blocks_of(g):
+            lead = PAIR * (g % ROUNDS_PER_CHUNK)
+            return range(lead, lead + PAIR)
+
+        def corner(g, b, parity, side):
+            return banks[(g, b, parity)][:].rearrange("p (n e) -> p e n", e=2)[:, side, :]
+
+        def convolve(g):
+            c = g // ROUNDS_PER_CHUNK
+            for b in blocks_of(g):
+                for parity in range(2):
+                    bank = new_bank()
+                    nc.tensor.matmul_mx(
+                        out=bank[:],
+                        lhsT=w_codes[:, b, :].bitcast(FP8X4),
+                        lhsT_scale=w_scales[:, b, :],
+                        rhs=x_codes[c][:, parity, :].bitcast(FP8X4),
+                        rhs_scale=x_scales[c][:, parity, :],
+                        start=True,
+                        stop=True,
+                    )
+                    banks[(g, b, parity)] = bank
+
+        def first_max(g):
+            for b in blocks_of(g):
+                opening = scratch.tile([P, POOLED], F32, name="opening", tag="opening")
+                nc.scalar.activation(
+                    out=opening[:], in_=corner(g, b, *FIRST_CORNER), func=IDENTITY, bias=bias[:, b : b + 1], scale=1.0
+                )
+                running[b] = opening[:]
+
+        def rest_max(g):
+            c = g // ROUNDS_PER_CHUNK
+            for parity, side in LATER_CORNERS:
+                for b in blocks_of(g):
+                    if (parity, side) == LATER_CORNERS[-1]:
+                        target = pooled[c][:, b, :]
+                    else:
+                        partial = scratch.tile([P, POOLED], F32, name="partial", tag="partial")
+                        target = partial[:]
+                    nc.vector.scalar_tensor_tensor(
+                        out=target,
+                        in0=corner(g, b, parity, side),
+                        scalar=bias[:, b : b + 1],
+                        in1=running[b],
+                        op0=ADD,
+                        op1=MAX,
+                    )
+                    running[b] = target
+
+        def turn_q(c):
+            bank = new_bank()
+            for s in range(POOLED // P):
+                nc.tensor.transpose(bank[:, s * P : (s + 1) * P], pooled[c][:, 0, s * P : (s + 1) * P], ident[:])
+            return bank
+
+        def store_q(c, bank):
+            nc.scalar.copy(out=q_rows[c][:].rearrange("n s o -> n (s o)"), in_=bank[:, 0:POOLED])
+            nc.sync.dma_start(out=q_out[:, c * (POOLED // P) : (c + 1) * (POOLED // P), :], in_=q_rows[c][:])
+
+        def store_round(g):
+            c, r = divmod(g, ROUNDS_PER_CHUNK)
+            positions = slice(c * POOLED, (c + 1) * POOLED)
+            if r == 0:
+                nc.sync.dma_start(out=k_out[:, positions], in_=pooled[c][:, 1, :])
+            else:
+                nc.sync.dma_start(
+                    out=v_out[:, PAIR * (r - 1) : PAIR * r, positions], in_=pooled[c][:, PAIR * r : PAIR * (r + 1), :]
+                )
+
+        make_identity(nc, ident[:])
+        nc.vector.memset(bias_rows[:], 0.0)
+        nc.sync.dma_start(out=w_rows[:, 0, :], in_=wq)
+        nc.sync.dma_start(out=w_rows[:, 1, :], in_=wk)
+        load_unit(0)
+        load_unit(1)
+        nc.sync.dma_start(out=bias_rows[0:1, :], in_=bq.rearrange("(r o) -> r o", r=1))
+        nc.sync.dma_start(out=bias_rows[1:2, :], in_=bk.rearrange("(r o) -> r o", r=1))
+        nc.sync.dma_start(out=bias_rows[2:BLOCKS, :], in_=bv.rearrange("(r o) -> r o", o=P))
+        nc.sync.dma_start(out=w_rows[:, 2:BLOCKS, :], in_=wv.rearrange("(b o) c -> o b c", o=P))
+        for u in range(2, PIXELS // UNIT):
+            load_unit(u)
+        nc.vector.memset(table_warmer[:, 0:1], 0.0)
+        nc.scalar.activation(out=table_warmer[:, 1:2], in_=table_warmer[:, 0:1], func=IDENTITY)
+
+        prepare_weights(0)
+        nc.vector.tensor_copy(out=bias_rows_f32[:], in_=bias_rows[:])
+        bias_bank = new_bank()
+        nc.tensor.transpose(bias_bank[:, 0:P], bias_rows_f32[:], ident[:])
+        nc.vector.tensor_copy(out=bias[:], in_=bias_bank[:, 0:BLOCKS])
+        regroup_unit(0)
+        regroup_unit(1)
+        quantise_chunk(0)
+        prepare_weights(2)
+        prepare_weights(4)
+        convolve(0)
+        first_max(0)
+
+        for g in range(ROUNDS):
+            c, r = divmod(g, ROUNDS_PER_CHUNK)
+            more_chunks = c + 1 < N_CHUNKS
+            if more_chunks and r < CHUNK // UNIT:
+                regroup_unit((c + 1) * (CHUNK // UNIT) + r)
+            if r == 1:
+                q_bank = turn_q(c)
+            if g + 1 < ROUNDS:
+                convolve(g + 1)
+                first_max(g + 1)
+            if r == 1:
+                store_q(c, q_bank)
+            rest_max(g)
+            if more_chunks and r == 1:
+                quantise_chunk(c + 1)
+            store_round(g)

@@ -37,6 +37,7 @@ def tile_selfattentionpatch_pa_kernel(tc, x, wq, bq, wk, bk, wv, bv, out_0, out_
     with ExitStack() as ctx:
         keep = ctx.enter_context(tc.tile_pool(name="keep", bufs=1))
         scratch = ctx.enter_context(tc.tile_pool(name="scratch", bufs=8))
+        turns = ctx.enter_context(tc.tile_pool(name="turns", bufs=1))
         psum = ctx.enter_context(tc.psum_pool(name="psum", bufs=8))
         ctx.enter_context(tc.manual_schedule())
 
@@ -55,10 +56,8 @@ def tile_selfattentionpatch_pa_kernel(tc, x, wq, bq, wk, bk, wv, bv, out_0, out_
         w_codes = keep.tile([P, BLOCKS, P], U32, align_bytes=64)
         w_scales = keep.tile([P, BLOCKS, P], U8, align_bytes=64)
         x_raw = [keep.tile([P, PACK, UNIT], BF16, name="x_raw%d" % u) for u in range(PIXELS // UNIT)]
-        x_grouped = [
-            keep.tile([P, 2, HALF, PACK], BF16, name="x_grouped%d" % c, align_bytes=64)
-            for c in range(N_CHUNKS)
-        ]
+        x_even = [keep.tile([P, HALF, PACK], BF16, name="x_even%d" % c, align_bytes=64) for c in range(N_CHUNKS)]
+        x_odd = {}
         x_codes = [keep.tile([P, 2, HALF], U32, name="x_codes%d" % c, align_bytes=64) for c in range(N_CHUNKS)]
         x_scales = [keep.tile([P, 2, HALF], U8, name="x_scales%d" % c, align_bytes=64) for c in range(N_CHUNKS)]
         pooled = [keep.tile([P, BLOCKS, POOLED], F32, name="pooled%d" % c) for c in range(N_CHUNKS)]
@@ -76,8 +75,10 @@ def tile_selfattentionpatch_pa_kernel(tc, x, wq, bq, wk, bk, wv, bv, out_0, out_
             c, h = divmod(u, CHUNK // UNIT)
             by_parity = x_raw[u][:].rearrange("p t (i d w) -> p d i w t", d=2, w=IMAGE_W)
             columns = slice(h * (UNIT // 2), (h + 1) * (UNIT // 2))
-            even = x_grouped[c][:, 0, columns, :].rearrange("p (i w) t -> p i w t", w=IMAGE_W)
-            odd = x_grouped[c][:, 1, columns, :].rearrange("p (i w) t -> p i w t", w=IMAGE_W)
+            if h == 0:
+                x_odd[c] = turns.tile([P, HALF, PACK], BF16, name="x_odd", tag="x_odd", align_bytes=64)
+            even = x_even[c][:, columns, :].rearrange("p (i w) t -> p i w t", w=IMAGE_W)
+            odd = x_odd[c][:, columns, :].rearrange("p (i w) t -> p i w t", w=IMAGE_W)
             nc.scalar.copy(out=even, in_=by_parity[:, 0])
             nc.gpsimd.tensor_scalar(out=odd, in0=by_parity[:, 1], scalar1=1.0, scalar2=0.0, op0=MULT, op1=ADD)
 
@@ -86,7 +87,7 @@ def tile_selfattentionpatch_pa_kernel(tc, x, wq, bq, wk, bk, wv, bv, out_0, out_
                 nc.vector.quantize_mx(
                     out=x_codes[c][:, parity, :].bitcast(FP8X4),
                     scales=x_scales[c][:, parity, :],
-                    in_=x_grouped[c][:, parity].rearrange("p n t -> p (n t)"),
+                    in_=(x_odd[c] if parity else x_even[c])[:].rearrange("p n t -> p (n t)"),
                 )
 
         def prepare_weights(lead):
@@ -157,6 +158,8 @@ def tile_selfattentionpatch_pa_kernel(tc, x, wq, bq, wk, bk, wv, bv, out_0, out_
                         op1=MAX,
                     )
                     running[b] = target
+                    if g == ROUNDS - 1 and (parity, side) == LATER_CORNERS[-1]:
+                        nc.sync.dma_start(out=v_out[:, b - 2, c * POOLED : (c + 1) * POOLED], in_=pooled[c][:, b, :])
 
         def turn_q(c):
             bank = new_bank()
@@ -180,13 +183,13 @@ def tile_selfattentionpatch_pa_kernel(tc, x, wq, bq, wk, bk, wv, bv, out_0, out_
 
         make_identity(nc, ident[:])
         nc.vector.memset(bias_rows[:], 0.0)
+        nc.sync.dma_start(out=bias_rows[0:1, :], in_=bq.rearrange("(r o) -> r o", r=1))
+        nc.sync.dma_start(out=bias_rows[1:2, :], in_=bk.rearrange("(r o) -> r o", r=1))
+        nc.sync.dma_start(out=bias_rows[2:BLOCKS, :], in_=bv.rearrange("(r o) -> r o", o=P))
         nc.sync.dma_start(out=w_rows[:, 0, :], in_=wq)
         nc.sync.dma_start(out=w_rows[:, 1, :], in_=wk)
         load_unit(0)
         load_unit(1)
-        nc.sync.dma_start(out=bias_rows[0:1, :], in_=bq.rearrange("(r o) -> r o", r=1))
-        nc.sync.dma_start(out=bias_rows[1:2, :], in_=bk.rearrange("(r o) -> r o", r=1))
-        nc.sync.dma_start(out=bias_rows[2:BLOCKS, :], in_=bv.rearrange("(r o) -> r o", o=P))
         nc.sync.dma_start(out=w_rows[:, 2:BLOCKS, :], in_=wv.rearrange("(b o) c -> o b c", o=P))
         for u in range(2, PIXELS // UNIT):
             load_unit(u)
@@ -221,4 +224,5 @@ def tile_selfattentionpatch_pa_kernel(tc, x, wq, bq, wk, bk, wv, bv, out_0, out_
             rest_max(g)
             if more_chunks and r == 1:
                 quantise_chunk(c + 1)
-            store_round(g)
+            if g < ROUNDS - 1:
+                store_round(g)

@@ -183,11 +183,11 @@ def tile_selfattentionpatch_pa_kernel(tc, x, wq, bq, wk, bk, wv, bv, out_0, out_
 
         make_identity(nc, ident[:])
         nc.vector.memset(bias_rows[:], 0.0)
+        nc.sync.dma_start(out=w_rows[:, 0, :], in_=wq)
+        nc.sync.dma_start(out=w_rows[:, 1, :], in_=wk)
         nc.sync.dma_start(out=bias_rows[0:1, :], in_=bq.rearrange("(r o) -> r o", r=1))
         nc.sync.dma_start(out=bias_rows[1:2, :], in_=bk.rearrange("(r o) -> r o", r=1))
         nc.sync.dma_start(out=bias_rows[2:BLOCKS, :], in_=bv.rearrange("(r o) -> r o", o=P))
-        nc.sync.dma_start(out=w_rows[:, 0, :], in_=wq)
-        nc.sync.dma_start(out=w_rows[:, 1, :], in_=wk)
         load_unit(0)
         load_unit(1)
         nc.sync.dma_start(out=w_rows[:, 2:BLOCKS, :], in_=wv.rearrange("(b o) c -> o b c", o=P))

@@ -185,12 +185,14 @@ def tile_selfattentionpatch_pa_kernel(tc, x, wq, bq, wk, bk, wv, bv, out_0, out_
         nc.vector.memset(bias_rows[:], 0.0)
         nc.sync.dma_start(out=w_rows[:, 0, :], in_=wq)
         nc.sync.dma_start(out=w_rows[:, 1, :], in_=wk)
+        load_unit(0)
         nc.sync.dma_start(out=bias_rows[0:1, :], in_=bq.rearrange("(r o) -> r o", r=1))
         nc.sync.dma_start(out=bias_rows[1:2, :], in_=bk.rearrange("(r o) -> r o", r=1))
         nc.sync.dma_start(out=bias_rows[2:BLOCKS, :], in_=bv.rearrange("(r o) -> r o", o=P))
-        load_unit(0)
         load_unit(1)
-        nc.sync.dma_start(out=w_rows[:, 2:BLOCKS, :], in_=wv.rearrange("(b o) c -> o b c", o=P))
+        wv_blocks = wv.rearrange("(b o) c -> o b c", o=P)
+        for lead in range(PAIR, BLOCKS, PAIR):
+            nc.sync.dma_start(out=w_rows[:, lead : lead + PAIR, :], in_=wv_blocks[:, lead - PAIR : lead, :])
         for u in range(2, PIXELS // UNIT):
             load_unit(u)
         nc.vector.memset(table_warmer[:, 0:1], 0.0)

@@ -82,8 +82,8 @@ def tile_selfattentionpatch_pa_kernel(tc, x, wq, bq, wk, bk, wv, bv, out_0, out_
             nc.scalar.copy(out=even, in_=by_parity[:, 0])
             nc.gpsimd.tensor_scalar(out=odd, in0=by_parity[:, 1], scalar1=1.0, scalar2=0.0, op0=MULT, op1=ADD)
 
-        def quantise_chunk(c):
-            for parity in range(2):
+        def quantise_chunk(c, parities=(0, 1)):
+            for parity in parities:
                 nc.vector.quantize_mx(
                     out=x_codes[c][:, parity, :].bitcast(FP8X4),
                     scales=x_scales[c][:, parity, :],
@@ -118,8 +118,8 @@ def tile_selfattentionpatch_pa_kernel(tc, x, wq, bq, wk, bk, wv, bv, out_0, out_
 
         def convolve(g):
             c = g // ROUNDS_PER_CHUNK
-            for b in blocks_of(g):
-                for parity in range(2):
+            for parity in range(2):
+                for b in blocks_of(g):
                     bank = new_bank()
                     nc.tensor.matmul_mx(
                         out=bank[:],
@@ -205,9 +205,10 @@ def tile_selfattentionpatch_pa_kernel(tc, x, wq, bq, wk, bk, wv, bv, out_0, out_
         nc.vector.tensor_copy(out=bias[:], in_=bias_bank[:, 0:BLOCKS])
         regroup_unit(0)
         regroup_unit(1)
-        quantise_chunk(0)
+        quantise_chunk(0, (0,))
         prepare_weights(2)
         prepare_weights(4)
+        quantise_chunk(0, (1,))
         convolve(0)
         first_max(0)
 

@@ -212,20 +212,24 @@ def tile_selfattentionpatch_pa_kernel(tc, x, wq, bq, wk, bk, wv, bv, out_0, out_
         convolve(0)
         first_max(0)
 
+        regroup_at = {0: 2, 1: 3}
+        quantise_at = {1: 1}
+        for c in range(2, N_CHUNKS):
+            opening_round = (c - 1) * ROUNDS_PER_CHUNK
+            for h in range(CHUNK // UNIT):
+                regroup_at[opening_round - 1 + h] = c * (CHUNK // UNIT) + h
+            quantise_at[opening_round] = c
         for g in range(ROUNDS):
             c, r = divmod(g, ROUNDS_PER_CHUNK)
-            more_chunks = c + 1 < N_CHUNKS
-            if more_chunks and r < CHUNK // UNIT:
-                regroup_unit((c + 1) * (CHUNK // UNIT) + r)
-            if r == 1:
-                q_bank = turn_q(c)
+            if g in regroup_at:
+                regroup_unit(regroup_at[g])
             if g + 1 < ROUNDS:
                 convolve(g + 1)
                 first_max(g + 1)
             if r == 1:
-                store_q(c, q_bank)
+                store_q(c, turn_q(c))
             rest_max(g)
-            if more_chunks and r == 1:
-                quantise_chunk(c + 1)
+            if g in quantise_at:
+                quantise_chunk(quantise_at[g])
             if g < ROUNDS - 1:
                 store_round(g)

@@ -12,6 +12,7 @@ ADD = mybir.AluOpType.add
 MULT = mybir.AluOpType.mult
 MAX = mybir.AluOpType.max
 IDENTITY = mybir.ActivationFunctionType.Identity
+RELU = mybir.ActivationFunctionType.Relu
 
 P = 128
 PACK = 4
@@ -25,7 +26,9 @@ POOLED = CHUNK // 4
 BLOCKS = 6
 PAIR = 2
 ROUNDS_PER_CHUNK = BLOCKS // PAIR
-ROUNDS = N_CHUNKS * ROUNDS_PER_CHUNK
+BY_DIFFERENCE = [BLOCKS - 2, BLOCKS - 1]
+LAST_CHUNK = N_CHUNKS - 1
+ROUNDS = N_CHUNKS * ROUNDS_PER_CHUNK - 1
 FIRST_CORNER = (0, 0)
 LATER_CORNERS = ((0, 1), (1, 0), (1, 1))
 
@@ -62,6 +65,10 @@ def tile_selfattentionpatch_pa_kernel(tc, x, wq, bq, wk, bk, wv, bv, out_0, out_
         x_scales = [keep.tile([P, 2, HALF], U8, name="x_scales%d" % c, align_bytes=64) for c in range(N_CHUNKS)]
         pooled = [keep.tile([P, BLOCKS, POOLED], F32, name="pooled%d" % c) for c in range(N_CHUNKS)]
         q_rows = [keep.tile([P, POOLED // P, P], F32, name="q_rows%d" % c) for c in range(N_CHUNKS)]
+        w_negative = keep.tile([P, PAIR, P, PACK], BF16, align_bytes=64)
+        w_negative_codes = keep.tile([P, PAIR, P], U32, align_bytes=64)
+        w_negative_scales = keep.tile([P, PAIR, P], U8, align_bytes=64)
+        row_max = {}
         banks = {}
         running = {}
 
@@ -143,6 +150,8 @@ def tile_selfattentionpatch_pa_kernel(tc, x, wq, bq, wk, bk, wv, bv, out_0, out_
         def rest_max(g):
             c = g // ROUNDS_PER_CHUNK
             for parity, side in LATER_CORNERS:
+                if g == ROUNDS - 1 and (parity, side) == LATER_CORNERS[-1]:
+                    merge_columns()
                 for b in blocks_of(g):
                     if (parity, side) == LATER_CORNERS[-1]:
                         target = pooled[c][:, b, :]
@@ -160,6 +169,52 @@ def tile_selfattentionpatch_pa_kernel(tc, x, wq, bq, wk, bk, wv, bv, out_0, out_
                     running[b] = target
                     if g == ROUNDS - 1 and (parity, side) == LATER_CORNERS[-1]:
                         nc.sync.dma_start(out=v_out[:, b - 2, c * POOLED : (c + 1) * POOLED], in_=pooled[c][:, b, :])
+
+        def negate_weights():
+            nc.gpsimd.tensor_scalar(
+                out=w_negative[:], in0=w_grouped[:, BLOCKS - 2 : BLOCKS], scalar1=-1.0, scalar2=0.0, op0=MULT, op1=ADD
+            )
+
+        def quantise_negative_weights():
+            nc.vector.quantize_mx(
+                out=w_negative_codes[:].rearrange("p b o -> p (b o)").bitcast(FP8X4),
+                scales=w_negative_scales[:].rearrange("p b o -> p (b o)"),
+                in_=w_negative[:].rearrange("p b o t -> p (b o t)"),
+            )
+
+        def one_pass(bank, codes, scales, parity, start, stop):
+            nc.tensor.matmul_mx(
+                out=bank[:],
+                lhsT=codes.bitcast(FP8X4),
+                lhsT_scale=scales,
+                rhs=x_codes[LAST_CHUNK][:, parity, :].bitcast(FP8X4),
+                rhs_scale=x_scales[LAST_CHUNK][:, parity, :],
+                start=start,
+                stop=stop,
+            )
+
+        def convolve_difference(j):
+            b = BY_DIFFERENCE[j]
+            difference = new_bank()
+            one_pass(difference, w_codes[:, b, :], w_scales[:, b, :], 0, True, False)
+            one_pass(difference, w_negative_codes[:, j, :], w_negative_scales[:, j, :], 1, False, True)
+            odd = new_bank()
+            one_pass(odd, w_codes[:, b, :], w_scales[:, b, :], 1, True, True)
+            rise = keep.tile([P, HALF], F32, name="rise%d" % j)
+            nc.scalar.activation(out=rise[:], in_=difference[:], func=RELU)
+            odd_rows = keep.tile([P, HALF], F32, name="odd_rows%d" % j)
+            nc.scalar.activation(out=odd_rows[:], in_=odd[:], func=IDENTITY, bias=bias[:, b : b + 1], scale=1.0)
+            row_max[b] = keep.tile([P, HALF], F32, name="row_max%d" % j)
+            nc.gpsimd.tensor_tensor(out=row_max[b][:], in0=rise[:], in1=odd_rows[:], op=ADD)
+
+        def merge_columns():
+            for b in BY_DIFFERENCE:
+                sides = row_max[b][:].rearrange("p (n e) -> p e n", e=2)
+                nc.vector.tensor_tensor(out=pooled[LAST_CHUNK][:, b, :], in0=sides[:, 0, :], in1=sides[:, 1, :], op=MAX)
+            positions = slice(LAST_CHUNK * POOLED, PIXELS // 4)
+            nc.sync.dma_start(
+                out=v_out[:, BLOCKS - PAIR - 2 : BLOCKS - 2, positions], in_=pooled[LAST_CHUNK][:, BLOCKS - PAIR : BLOCKS, :]
+            )
 
         def turn_q(c):
             bank = new_bank()
@@ -223,13 +278,20 @@ def tile_selfattentionpatch_pa_kernel(tc, x, wq, bq, wk, bk, wv, bv, out_0, out_
             c, r = divmod(g, ROUNDS_PER_CHUNK)
             if g in regroup_at:
                 regroup_unit(regroup_at[g])
+                if regroup_at[g] == PIXELS // UNIT - 1:
+                    negate_weights()
             if g + 1 < ROUNDS:
                 convolve(g + 1)
                 first_max(g + 1)
             if r == 1:
                 store_q(c, turn_q(c))
+            if g in (ROUNDS - 4, ROUNDS - 3):
+                convolve_difference(g - (ROUNDS - 4))
             rest_max(g)
             if g in quantise_at:
-                quantise_chunk(quantise_at[g])
+                quantise_chunk(quantise_at[g], (0,))
+                if quantise_at[g] == LAST_CHUNK:
+                    quantise_negative_weights()
+                quantise_chunk(quantise_at[g], (1,))
             if g < ROUNDS - 1:
                 store_round(g)

@@ -24,11 +24,18 @@ N_CHUNKS = PIXELS // CHUNK
 HALF = CHUNK // 2
 POOLED = CHUNK // 4
 BLOCKS = 6
+N_BANKS = 8
 PAIR = 2
 ROUNDS_PER_CHUNK = BLOCKS // PAIR
 BY_DIFFERENCE = [BLOCKS - 2, BLOCKS - 1]
 LAST_CHUNK = N_CHUNKS - 1
-ROUNDS = N_CHUNKS * ROUNDS_PER_CHUNK - 1
+ROUNDS = [
+    (c, lead)
+    for c in range(N_CHUNKS)
+    for lead in range(0, BLOCKS, PAIR)
+    if c < LAST_CHUNK - 1 or lead != BY_DIFFERENCE[0]
+]
+FINAL = len(ROUNDS) - 1
 FIRST_CORNER = (0, 0)
 LATER_CORNERS = ((0, 1), (1, 0), (1, 1))
 
@@ -41,7 +48,7 @@ def tile_selfattentionpatch_pa_kernel(tc, x, wq, bq, wk, bk, wv, bv, out_0, out_
         keep = ctx.enter_context(tc.tile_pool(name="keep", bufs=1))
         scratch = ctx.enter_context(tc.tile_pool(name="scratch", bufs=8))
         turns = ctx.enter_context(tc.tile_pool(name="turns", bufs=1))
-        psum = ctx.enter_context(tc.psum_pool(name="psum", bufs=8))
+        psum = ctx.enter_context(tc.psum_pool(name="psum", bufs=1))
         ctx.enter_context(tc.manual_schedule())
 
         x_rows = x[0].rearrange("(p t) h w -> p t (h w)", t=PACK)
@@ -68,12 +75,17 @@ def tile_selfattentionpatch_pa_kernel(tc, x, wq, bq, wk, bk, wv, bv, out_0, out_
         w_negative = keep.tile([P, PAIR, P, PACK], BF16, align_bytes=64)
         w_negative_codes = keep.tile([P, PAIR, P], U32, align_bytes=64)
         w_negative_scales = keep.tile([P, PAIR, P], U8, align_bytes=64)
+        turn = []
+        copies = {}
         row_max = {}
         banks = {}
         running = {}
 
-        def new_bank():
-            return psum.tile([P, HALF], F32, name="bank", tag="bank")
+        def new_bank(k=None):
+            if k is None:
+                k = len(turn) % N_BANKS
+                turn.append(k)
+            return psum.tile([P, HALF], F32, name="bank%d" % k, tag="bank%d" % k)
 
         def load_unit(u):
             nc.sync.dma_start(out=x_raw[u][:], in_=x_rows[:, :, u * UNIT : (u + 1) * UNIT])
@@ -117,17 +129,18 @@ def tile_selfattentionpatch_pa_kernel(tc, x, wq, bq, wk, bk, wv, bv, out_0, out_
             )
 
         def blocks_of(g):
-            lead = PAIR * (g % ROUNDS_PER_CHUNK)
+            lead = ROUNDS[g][1]
             return range(lead, lead + PAIR)
 
         def corner(g, b, parity, side):
             return banks[(g, b, parity)][:].rearrange("p (n e) -> p e n", e=2)[:, side, :]
 
-        def convolve(g):
-            c = g // ROUNDS_PER_CHUNK
-            for parity in range(2):
+        def convolve(g, parities=(0, 1), given=()):
+            c = ROUNDS[g][0]
+            given = list(given)
+            for parity in parities:
                 for b in blocks_of(g):
-                    bank = new_bank()
+                    bank = new_bank(given.pop(0)) if given else new_bank()
                     nc.tensor.matmul_mx(
                         out=bank[:],
                         lhsT=w_codes[:, b, :].bitcast(FP8X4),
@@ -148,10 +161,10 @@ def tile_selfattentionpatch_pa_kernel(tc, x, wq, bq, wk, bk, wv, bv, out_0, out_
                 running[b] = opening[:]
 
         def rest_max(g):
-            c = g // ROUNDS_PER_CHUNK
+            c = ROUNDS[g][0]
             for parity, side in LATER_CORNERS:
-                if g == ROUNDS - 1 and (parity, side) == LATER_CORNERS[-1]:
-                    merge_columns()
+                if g == FINAL and (parity, side) == LATER_CORNERS[1]:
+                    merge_columns(LAST_CHUNK, 1)
                 for b in blocks_of(g):
                     if (parity, side) == LATER_CORNERS[-1]:
                         target = pooled[c][:, b, :]
@@ -167,12 +180,12 @@ def tile_selfattentionpatch_pa_kernel(tc, x, wq, bq, wk, bk, wv, bv, out_0, out_
                         op1=MAX,
                     )
                     running[b] = target
-                    if g == ROUNDS - 1 and (parity, side) == LATER_CORNERS[-1]:
+                    if g == FINAL and (parity, side) == LATER_CORNERS[-1]:
                         nc.sync.dma_start(out=v_out[:, b - 2, c * POOLED : (c + 1) * POOLED], in_=pooled[c][:, b, :])
 
         def negate_weights():
-            nc.gpsimd.tensor_scalar(
-                out=w_negative[:], in0=w_grouped[:, BLOCKS - 2 : BLOCKS], scalar1=-1.0, scalar2=0.0, op0=MULT, op1=ADD
+            nc.vector.tensor_scalar(
+                out=w_negative[:], in0=w_grouped[:, BLOCKS - 2 : BLOCKS], scalar1=-1.0, scalar2=None, op0=MULT
             )
 
         def quantise_negative_weights():
@@ -182,42 +195,49 @@ def tile_selfattentionpatch_pa_kernel(tc, x, wq, bq, wk, bk, wv, bv, out_0, out_
                 in_=w_negative[:].rearrange("p b o t -> p (b o t)"),
             )
 
-        def one_pass(bank, codes, scales, parity, start, stop):
-            nc.tensor.matmul_mx(
-                out=bank[:],
-                lhsT=codes.bitcast(FP8X4),
-                lhsT_scale=scales,
-                rhs=x_codes[LAST_CHUNK][:, parity, :].bitcast(FP8X4),
-                rhs_scale=x_scales[LAST_CHUNK][:, parity, :],
-                start=start,
-                stop=stop,
-            )
-
-        def convolve_difference(j):
+        def convolve_difference(c, j, given):
             b = BY_DIFFERENCE[j]
-            difference = new_bank()
-            one_pass(difference, w_codes[:, b, :], w_scales[:, b, :], 0, True, False)
-            one_pass(difference, w_negative_codes[:, j, :], w_negative_scales[:, j, :], 1, False, True)
-            odd = new_bank()
-            one_pass(odd, w_codes[:, b, :], w_scales[:, b, :], 1, True, True)
-            rise = keep.tile([P, HALF], F32, name="rise%d" % j)
+            difference, odd = new_bank(given[0]), new_bank(given[1])
+            negative = (w_negative_codes[:, j, :], w_negative_scales[:, j, :])
+            positive = (w_codes[:, b, :], w_scales[:, b, :])
+            for bank, (codes, scales), parity, start, stop in (
+                (difference, positive, 0, True, False),
+                (difference, negative, 1, False, True),
+                (odd, positive, 1, True, True),
+            ):
+                nc.tensor.matmul_mx(
+                    out=bank[:],
+                    lhsT=codes.bitcast(FP8X4),
+                    lhsT_scale=scales,
+                    rhs=x_codes[c][:, parity, :].bitcast(FP8X4),
+                    rhs_scale=x_scales[c][:, parity, :],
+                    start=start,
+                    stop=stop,
+                )
+            rise = scratch.tile([P, HALF], F32, name="rise", tag="rise")
             nc.scalar.activation(out=rise[:], in_=difference[:], func=RELU)
-            odd_rows = keep.tile([P, HALF], F32, name="odd_rows%d" % j)
+            odd_rows = scratch.tile([P, HALF], F32, name="odd_rows", tag="odd_rows")
             nc.scalar.activation(out=odd_rows[:], in_=odd[:], func=IDENTITY, bias=bias[:, b : b + 1], scale=1.0)
-            row_max[b] = keep.tile([P, HALF], F32, name="row_max%d" % j)
-            nc.gpsimd.tensor_tensor(out=row_max[b][:], in0=rise[:], in1=odd_rows[:], op=ADD)
+            copies[c, b] = (rise, odd_rows)
 
-        def merge_columns():
-            for b in BY_DIFFERENCE:
-                sides = row_max[b][:].rearrange("p (n e) -> p e n", e=2)
-                nc.vector.tensor_tensor(out=pooled[LAST_CHUNK][:, b, :], in0=sides[:, 0, :], in1=sides[:, 1, :], op=MAX)
-            positions = slice(LAST_CHUNK * POOLED, PIXELS // 4)
-            nc.sync.dma_start(
-                out=v_out[:, BLOCKS - PAIR - 2 : BLOCKS - 2, positions], in_=pooled[LAST_CHUNK][:, BLOCKS - PAIR : BLOCKS, :]
-            )
+        def add_difference(c, j):
+            b = BY_DIFFERENCE[j]
+            rise, odd_rows = copies[c, b]
+            if (c, j) == (LAST_CHUNK - 1, 0):
+                total = turns.tile([P, HALF], F32, name="total", tag="x_odd", align_bytes=64)
+            else:
+                total = scratch.tile([P, HALF], F32, name="row_max", tag="row_max")
+            nc.gpsimd.tensor_tensor(out=total[:], in0=rise[:], in1=odd_rows[:], op=ADD)
+            row_max[c, b] = total
 
-        def turn_q(c):
-            bank = new_bank()
+        def merge_columns(c, j):
+            b = BY_DIFFERENCE[j]
+            sides = row_max[c, b][:].rearrange("p (n e) -> p e n", e=2)
+            nc.vector.tensor_tensor(out=pooled[c][:, b, :], in0=sides[:, 0, :], in1=sides[:, 1, :], op=MAX)
+            nc.sync.dma_start(out=v_out[:, b - 2, c * POOLED : (c + 1) * POOLED], in_=pooled[c][:, b, :])
+
+        def turn_q(c, k=None):
+            bank = new_bank(k)
             for s in range(POOLED // P):
                 nc.tensor.transpose(bank[:, s * P : (s + 1) * P], pooled[c][:, 0, s * P : (s + 1) * P], ident[:])
             return bank
@@ -227,7 +247,8 @@ def tile_selfattentionpatch_pa_kernel(tc, x, wq, bq, wk, bk, wv, bv, out_0, out_
             nc.sync.dma_start(out=q_out[:, c * (POOLED // P) : (c + 1) * (POOLED // P), :], in_=q_rows[c][:])
 
         def store_round(g):
-            c, r = divmod(g, ROUNDS_PER_CHUNK)
+            c, lead = ROUNDS[g]
+            r = lead // PAIR
             positions = slice(c * POOLED, (c + 1) * POOLED)
             if r == 0:
                 nc.sync.dma_start(out=k_out[:, positions], in_=pooled[c][:, 1, :])
@@ -267,31 +288,52 @@ def tile_selfattentionpatch_pa_kernel(tc, x, wq, bq, wk, bk, wv, bv, out_0, out_
         convolve(0)
         first_max(0)
 
-        regroup_at = {0: 2, 1: 3}
-        quantise_at = {1: 1}
-        for c in range(2, N_CHUNKS):
-            opening_round = (c - 1) * ROUNDS_PER_CHUNK
-            for h in range(CHUNK // UNIT):
-                regroup_at[opening_round - 1 + h] = c * (CHUNK // UNIT) + h
-            quantise_at[opening_round] = c
-        for g in range(ROUNDS):
-            c, r = divmod(g, ROUNDS_PER_CHUNK)
-            if g in regroup_at:
-                regroup_unit(regroup_at[g])
-                if regroup_at[g] == PIXELS // UNIT - 1:
-                    negate_weights()
-            if g + 1 < ROUNDS:
+        regroup_at = {0: [2], 1: [3], 2: [4], 3: [5]}
+        spare, pairs = [], []
+        difference_at = {4: (2, 0), 5: (2, 1), 6: (3, 0), 7: (3, 1)}
+        for g in range(len(ROUNDS)):
+            c, lead = ROUNDS[g]
+            for u in regroup_at.get(g, ()):
+                regroup_unit(u)
+            if g == 5:
+                regroup_unit(7)
+                add_difference(2, 0)
+            if g == 8:
+                merge_columns(2, 0)
+                merge_columns(2, 1)
+                merge_columns(3, 0)
+            if g < 4:
                 convolve(g + 1)
                 first_max(g + 1)
-            if r == 1:
-                store_q(c, turn_q(c))
-            if g in (ROUNDS - 4, ROUNDS - 3):
-                convolve_difference(g - (ROUNDS - 4))
+            elif g < FINAL:
+                convolve(g + 1, (0,), pairs[2 * (g - 4) % 3])
+                first_max(g + 1)
+                if g == 7:
+                    store_q(2, turn_q(2, spare[0]))
+                if g in difference_at:
+                    convolve_difference(*difference_at[g], spare)
+                    if g > 4:
+                        add_difference(*difference_at[g])
+                convolve(g + 1, (1,), pairs[(2 * (g - 4) + 1) % 3])
+            if g == 1:
+                store_q(0, turn_q(0))
+            if g == 3:
+                regroup_unit(6)
+            if g == FINAL:
+                store_q(3, turn_q(3, spare[0]))
             rest_max(g)
-            if g in quantise_at:
-                quantise_chunk(quantise_at[g], (0,))
-                if quantise_at[g] == LAST_CHUNK:
-                    quantise_negative_weights()
-                quantise_chunk(quantise_at[g], (1,))
-            if g < ROUNDS - 1:
+            if g == 1:
+                quantise_chunk(1)
+            if g == 3:
+                banks_in_turn = [(len(turn) - N_BANKS + i) % N_BANKS for i in range(N_BANKS)]
+                spare = banks_in_turn[0:2]
+                pairs = [banks_in_turn[i : i + 2] for i in (2, 4, 6)]
+                store_q(1, turn_q(1, spare[0]))
+                negate_weights()
+                quantise_chunk(2, (0,))
+                quantise_negative_weights()
+                quantise_chunk(2, (1,))
+            if g == 5:
+                quantise_chunk(3)
+            if g < FINAL:
                 store_round(g)

@@ -76,6 +76,7 @@ def tile_selfattentionpatch_pa_kernel(tc, x, wq, bq, wk, bk, wv, bv, out_0, out_
         w_negative_codes = keep.tile([P, PAIR, P], U32, align_bytes=64)
         w_negative_scales = keep.tile([P, PAIR, P], U8, align_bytes=64)
         turn = []
+        merge_at = {8: [(2, 0), (2, 1), (3, 0)], 9: [(3, 1)]}
         copies = {}
         row_max = {}
         banks = {}
@@ -98,8 +99,13 @@ def tile_selfattentionpatch_pa_kernel(tc, x, wq, bq, wk, bk, wv, bv, out_0, out_
                 x_odd[c] = turns.tile([P, HALF, PACK], BF16, name="x_odd", tag="x_odd", align_bytes=64)
             even = x_even[c][:, columns, :].rearrange("p (i w) t -> p i w t", w=IMAGE_W)
             odd = x_odd[c][:, columns, :].rearrange("p (i w) t -> p i w t", w=IMAGE_W)
-            nc.scalar.copy(out=even, in_=by_parity[:, 0])
+            scalar_rows = UNIT // IMAGE_W // (4 if u == PIXELS // UNIT - 1 else 2)
+            nc.scalar.copy(out=even[:, 0:scalar_rows], in_=by_parity[:, 0, 0:scalar_rows])
             nc.gpsimd.tensor_scalar(out=odd, in0=by_parity[:, 1], scalar1=1.0, scalar2=0.0, op0=MULT, op1=ADD)
+            if scalar_rows < UNIT // IMAGE_W // 2:
+                nc.gpsimd.tensor_scalar(
+                    out=even[:, scalar_rows:], in0=by_parity[:, 0, scalar_rows:], scalar1=1.0, scalar2=0.0, op0=MULT, op1=ADD
+                )
 
         def quantise_chunk(c, parities=(0, 1)):
             for parity in parities:
@@ -163,8 +169,9 @@ def tile_selfattentionpatch_pa_kernel(tc, x, wq, bq, wk, bk, wv, bv, out_0, out_
         def rest_max(g):
             c = ROUNDS[g][0]
             for parity, side in LATER_CORNERS:
-                if g == FINAL and (parity, side) == LATER_CORNERS[1]:
-                    merge_columns(LAST_CHUNK, 1)
+                if (parity, side) == LATER_CORNERS[-1]:
+                    for c_of_merge, j in merge_at.get(g, ()):
+                        merge_columns(c_of_merge, j)
                 for b in blocks_of(g):
                     if (parity, side) == LATER_CORNERS[-1]:
                         target = pooled[c][:, b, :]
@@ -298,10 +305,6 @@ def tile_selfattentionpatch_pa_kernel(tc, x, wq, bq, wk, bk, wv, bv, out_0, out_
             if g == 5:
                 regroup_unit(7)
                 add_difference(2, 0)
-            if g == 8:
-                merge_columns(2, 0)
-                merge_columns(2, 1)
-                merge_columns(3, 0)
             if g < 4:
                 convolve(g + 1)
                 first_max(g + 1)
@@ -310,11 +313,13 @@ def tile_selfattentionpatch_pa_kernel(tc, x, wq, bq, wk, bk, wv, bv, out_0, out_
                 first_max(g + 1)
                 if g == 7:
                     store_q(2, turn_q(2, spare[0]))
+                    convolve(g + 1, (1,), pairs[(2 * (g - 4) + 1) % 3])
                 if g in difference_at:
                     convolve_difference(*difference_at[g], spare)
                     if g > 4:
                         add_difference(*difference_at[g])
-                convolve(g + 1, (1,), pairs[(2 * (g - 4) + 1) % 3])
+                if g != 7:
+                    convolve(g + 1, (1,), pairs[(2 * (g - 4) + 1) % 3])
             if g == 1:
                 store_q(0, turn_q(0))
             if g == 3:

from contextlib import ExitStack

import concourse.mybir as mybir
from concourse.masks import make_identity

F32 = mybir.dt.float32
BF16 = mybir.dt.bfloat16
U32 = mybir.dt.uint32
U8 = mybir.dt.uint8
FP8X4 = mybir.dt.float8_e4m3fn_x4
ADD = mybir.AluOpType.add
MULT = mybir.AluOpType.mult
MAX = mybir.AluOpType.max
IDENTITY = mybir.ActivationFunctionType.Identity
RELU = mybir.ActivationFunctionType.Relu

P = 128
PACK = 4
IMAGE_W = 64
PIXELS = 64 * IMAGE_W
UNIT = 8 * IMAGE_W
CHUNK = 2 * UNIT
N_CHUNKS = PIXELS // CHUNK
HALF = CHUNK // 2
POOLED = CHUNK // 4
BLOCKS = 6
N_BANKS = 8
PAIR = 2
ROUNDS_PER_CHUNK = BLOCKS // PAIR
BY_DIFFERENCE = [BLOCKS - 2, BLOCKS - 1]
LAST_CHUNK = N_CHUNKS - 1
ROUNDS = [
    (c, lead)
    for c in range(N_CHUNKS)
    for lead in range(0, BLOCKS, PAIR)
    if c < LAST_CHUNK - 1 or lead != BY_DIFFERENCE[0]
]
FINAL = len(ROUNDS) - 1
FIRST_CORNER = (0, 0)
LATER_CORNERS = ((0, 1), (1, 0), (1, 1))

FLOPS = 2 * BLOCKS * P * PACK * P * PIXELS


def tile_selfattentionpatch_pa_kernel(tc, x, wq, bq, wk, bk, wv, bv, out_0, out_1, out_2):
    nc = tc.nc
    with ExitStack() as ctx:
        keep = ctx.enter_context(tc.tile_pool(name="keep", bufs=1))
        scratch = ctx.enter_context(tc.tile_pool(name="scratch", bufs=8))
        turns = ctx.enter_context(tc.tile_pool(name="turns", bufs=1))
        psum = ctx.enter_context(tc.psum_pool(name="psum", bufs=1))
        ctx.enter_context(tc.manual_schedule())

        x_rows = x[0].rearrange("(p t) h w -> p t (h w)", t=PACK)
        q_out = out_0[0].rearrange("(s n) o -> n s o", n=P)
        k_out = out_1[0]
        v_out = out_2[0].rearrange("(b o) n -> o b n", o=P)

        ident = keep.tile([P, P], F32)
        table_warmer = keep.tile([P, 2], F32)
        bias_rows = keep.tile([P, P], BF16)
        bias_rows_f32 = keep.tile([P, P], F32)
        bias = keep.tile([P, BLOCKS], F32)
        w_rows = keep.tile([P, BLOCKS, PACK * P], BF16)
        w_grouped = keep.tile([P, BLOCKS, P, PACK], BF16, align_bytes=64)
        w_codes = keep.tile([P, BLOCKS, P], U32, align_bytes=64)
        w_scales = keep.tile([P, BLOCKS, P], U8, align_bytes=64)
        x_raw = [keep.tile([P, PACK, UNIT], BF16, name="x_raw%d" % u) for u in range(PIXELS // UNIT)]
        x_even = [keep.tile([P, HALF, PACK], BF16, name="x_even%d" % c, align_bytes=64) for c in range(N_CHUNKS)]
        x_odd = {}
        x_codes = [keep.tile([P, 2, HALF], U32, name="x_codes%d" % c, align_bytes=64) for c in range(N_CHUNKS)]
        x_scales = [keep.tile([P, 2, HALF], U8, name="x_scales%d" % c, align_bytes=64) for c in range(N_CHUNKS)]
        pooled = [keep.tile([P, BLOCKS, POOLED], F32, name="pooled%d" % c) for c in range(N_CHUNKS)]
        q_rows = [keep.tile([P, POOLED // P, P], F32, name="q_rows%d" % c) for c in range(N_CHUNKS)]
        w_negative = keep.tile([P, PAIR, P, PACK], BF16, align_bytes=64)
        w_negative_codes = keep.tile([P, PAIR, P], U32, align_bytes=64)
        w_negative_scales = keep.tile([P, PAIR, P], U8, align_bytes=64)
        turn = []
        merge_at = {8: [(2, 0), (2, 1), (3, 0)], 9: [(3, 1)]}
        copies = {}
        row_max = {}
        banks = {}
        running = {}

        def new_bank(k=None):
            if k is None:
                k = len(turn) % N_BANKS
                turn.append(k)
            return psum.tile([P, HALF], F32, name="bank%d" % k, tag="bank%d" % k)

        def load_unit(u):
            nc.sync.dma_start(out=x_raw[u][:], in_=x_rows[:, :, u * UNIT : (u + 1) * UNIT])

        def regroup_unit(u):
            c, h = divmod(u, CHUNK // UNIT)
            by_parity = x_raw[u][:].rearrange("p t (i d w) -> p d i w t", d=2, w=IMAGE_W)
            columns = slice(h * (UNIT // 2), (h + 1) * (UNIT // 2))
            if h == 0:
                x_odd[c] = turns.tile([P, HALF, PACK], BF16, name="x_odd", tag="x_odd", align_bytes=64)
            even = x_even[c][:, columns, :].rearrange("p (i w) t -> p i w t", w=IMAGE_W)
            odd = x_odd[c][:, columns, :].rearrange("p (i w) t -> p i w t", w=IMAGE_W)
            scalar_rows = UNIT // IMAGE_W // (4 if u == PIXELS // UNIT - 1 else 2)
            nc.scalar.copy(out=even[:, 0:scalar_rows], in_=by_parity[:, 0, 0:scalar_rows])
            nc.gpsimd.tensor_scalar(out=odd, in0=by_parity[:, 1], scalar1=1.0, scalar2=0.0, op0=MULT, op1=ADD)
            if scalar_rows < UNIT // IMAGE_W // 2:
                nc.gpsimd.tensor_scalar(
                    out=even[:, scalar_rows:], in0=by_parity[:, 0, scalar_rows:], scalar1=1.0, scalar2=0.0, op0=MULT, op1=ADD
                )

        def quantise_chunk(c, parities=(0, 1)):
            for parity in parities:
                nc.vector.quantize_mx(
                    out=x_codes[c][:, parity, :].bitcast(FP8X4),
                    scales=x_scales[c][:, parity, :],
                    in_=(x_odd[c] if parity else x_even[c])[:].rearrange("p n t -> p (n t)"),
                )

        def prepare_weights(lead):
            words = w_rows[:].bitcast(F32).rearrange("o b (p u) -> o b u p", u=2)
            bank = new_bank()
            for j in range(PAIR):
                for u in range(2):
                    nc.tensor.transpose(
                        bank[:, (2 * j + u) * P : (2 * j + u + 1) * P], words[:, lead + j, u, :], ident[:]
                    )
            both = slice(lead, lead + PAIR)
            nc.scalar.copy(
                out=w_grouped[:].bitcast(F32)[:, both],
                in_=bank[:].rearrange("p (j u o) -> p j o u", j=PAIR, u=2),
            )
            nc.vector.quantize_mx(
                out=w_codes[:, both, :].rearrange("p b o -> p (b o)").bitcast(FP8X4),
                scales=w_scales[:, both, :].rearrange("p b o -> p (b o)"),
                in_=w_grouped[:, both].rearrange("p b o t -> p (b o t)"),
            )

        def blocks_of(g):
            lead = ROUNDS[g][1]
            return range(lead, lead + PAIR)

        def corner(g, b, parity, side):
            return banks[(g, b, parity)][:].rearrange("p (n e) -> p e n", e=2)[:, side, :]

        def convolve(g, parities=(0, 1), given=()):
            c = ROUNDS[g][0]
            given = list(given)
            for parity in parities:
                for b in blocks_of(g):
                    bank = new_bank(given.pop(0)) if given else new_bank()
                    nc.tensor.matmul_mx(
                        out=bank[:],
                        lhsT=w_codes[:, b, :].bitcast(FP8X4),
                        lhsT_scale=w_scales[:, b, :],
                        rhs=x_codes[c][:, parity, :].bitcast(FP8X4),
                        rhs_scale=x_scales[c][:, parity, :],
                        start=True,
                        stop=True,
                    )
                    banks[(g, b, parity)] = bank

        def first_max(g):
            for b in blocks_of(g):
                opening = scratch.tile([P, POOLED], F32, name="opening", tag="opening")
                nc.scalar.activation(
                    out=opening[:], in_=corner(g, b, *FIRST_CORNER), func=IDENTITY, bias=bias[:, b : b + 1], scale=1.0
                )
                running[b] = opening[:]

        def rest_max(g):
            c = ROUNDS[g][0]
            for parity, side in LATER_CORNERS:
                if (parity, side) == LATER_CORNERS[-1]:
                    for c_of_merge, j in merge_at.get(g, ()):
                        merge_columns(c_of_merge, j)
                for b in blocks_of(g):
                    if (parity, side) == LATER_CORNERS[-1]:
                        target = pooled[c][:, b, :]
                    else:
                        partial = scratch.tile([P, POOLED], F32, name="partial", tag="partial")
                        target = partial[:]
                    nc.vector.scalar_tensor_tensor(
                        out=target,
                        in0=corner(g, b, parity, side),
                        scalar=bias[:, b : b + 1],
                        in1=running[b],
                        op0=ADD,
                        op1=MAX,
                    )
                    running[b] = target
                    if g == FINAL and (parity, side) == LATER_CORNERS[-1]:
                        nc.sync.dma_start(out=v_out[:, b - 2, c * POOLED : (c + 1) * POOLED], in_=pooled[c][:, b, :])

        def negate_weights():
            nc.vector.tensor_scalar(
                out=w_negative[:], in0=w_grouped[:, BLOCKS - 2 : BLOCKS], scalar1=-1.0, scalar2=None, op0=MULT
            )

        def quantise_negative_weights():
            nc.vector.quantize_mx(
                out=w_negative_codes[:].rearrange("p b o -> p (b o)").bitcast(FP8X4),
                scales=w_negative_scales[:].rearrange("p b o -> p (b o)"),
                in_=w_negative[:].rearrange("p b o t -> p (b o t)"),
            )

        def convolve_difference(c, j, given):
            b = BY_DIFFERENCE[j]
            difference, odd = new_bank(given[0]), new_bank(given[1])
            negative = (w_negative_codes[:, j, :], w_negative_scales[:, j, :])
            positive = (w_codes[:, b, :], w_scales[:, b, :])
            for bank, (codes, scales), parity, start, stop in (
                (difference, positive, 0, True, False),
                (difference, negative, 1, False, True),
                (odd, positive, 1, True, True),
            ):
                nc.tensor.matmul_mx(
                    out=bank[:],
                    lhsT=codes.bitcast(FP8X4),
                    lhsT_scale=scales,
                    rhs=x_codes[c][:, parity, :].bitcast(FP8X4),
                    rhs_scale=x_scales[c][:, parity, :],
                    start=start,
                    stop=stop,
                )
            rise = scratch.tile([P, HALF], F32, name="rise", tag="rise")
            nc.scalar.activation(out=rise[:], in_=difference[:], func=RELU)
            odd_rows = scratch.tile([P, HALF], F32, name="odd_rows", tag="odd_rows")
            nc.scalar.activation(out=odd_rows[:], in_=odd[:], func=IDENTITY, bias=bias[:, b : b + 1], scale=1.0)
            copies[c, b] = (rise, odd_rows)

        def add_difference(c, j):
            b = BY_DIFFERENCE[j]
            rise, odd_rows = copies[c, b]
            if (c, j) == (LAST_CHUNK - 1, 0):
                total = turns.tile([P, HALF], F32, name="total", tag="x_odd", align_bytes=64)
            else:
                total = scratch.tile([P, HALF], F32, name="row_max", tag="row_max")
            nc.gpsimd.tensor_tensor(out=total[:], in0=rise[:], in1=odd_rows[:], op=ADD)
            row_max[c, b] = total

        def merge_columns(c, j):
            b = BY_DIFFERENCE[j]
            sides = row_max[c, b][:].rearrange("p (n e) -> p e n", e=2)
            nc.vector.tensor_tensor(out=pooled[c][:, b, :], in0=sides[:, 0, :], in1=sides[:, 1, :], op=MAX)
            nc.sync.dma_start(out=v_out[:, b - 2, c * POOLED : (c + 1) * POOLED], in_=pooled[c][:, b, :])

        def turn_q(c, k=None):
            bank = new_bank(k)
            for s in range(POOLED // P):
                nc.tensor.transpose(bank[:, s * P : (s + 1) * P], pooled[c][:, 0, s * P : (s + 1) * P], ident[:])
            return bank

        def store_q(c, bank):
            nc.scalar.copy(out=q_rows[c][:].rearrange("n s o -> n (s o)"), in_=bank[:, 0:POOLED])
            nc.sync.dma_start(out=q_out[:, c * (POOLED // P) : (c + 1) * (POOLED // P), :], in_=q_rows[c][:])

        def store_round(g):
            c, lead = ROUNDS[g]
            r = lead // PAIR
            positions = slice(c * POOLED, (c + 1) * POOLED)
            if r == 0:
                nc.sync.dma_start(out=k_out[:, positions], in_=pooled[c][:, 1, :])
            else:
                nc.sync.dma_start(
                    out=v_out[:, PAIR * (r - 1) : PAIR * r, positions], in_=pooled[c][:, PAIR * r : PAIR * (r + 1), :]
                )

        make_identity(nc, ident[:])
        nc.vector.memset(bias_rows[:], 0.0)
        nc.sync.dma_start(out=w_rows[:, 0, :], in_=wq)
        nc.sync.dma_start(out=w_rows[:, 1, :], in_=wk)
        load_unit(0)
        nc.sync.dma_start(out=bias_rows[0:1, :], in_=bq.rearrange("(r o) -> r o", r=1))
        nc.sync.dma_start(out=bias_rows[1:2, :], in_=bk.rearrange("(r o) -> r o", r=1))
        nc.sync.dma_start(out=bias_rows[2:BLOCKS, :], in_=bv.rearrange("(r o) -> r o", o=P))
        load_unit(1)
        wv_blocks = wv.rearrange("(b o) c -> o b c", o=P)
        for lead in range(PAIR, BLOCKS, PAIR):
            nc.sync.dma_start(out=w_rows[:, lead : lead + PAIR, :], in_=wv_blocks[:, lead - PAIR : lead, :])
        for u in range(2, PIXELS // UNIT):
            load_unit(u)
        nc.vector.memset(table_warmer[:, 0:1], 0.0)
        nc.scalar.activation(out=table_warmer[:, 1:2], in_=table_warmer[:, 0:1], func=IDENTITY)

        prepare_weights(0)
        nc.vector.tensor_copy(out=bias_rows_f32[:], in_=bias_rows[:])
        bias_bank = new_bank()
        nc.tensor.transpose(bias_bank[:, 0:P], bias_rows_f32[:], ident[:])
        nc.vector.tensor_copy(out=bias[:], in_=bias_bank[:, 0:BLOCKS])
        regroup_unit(0)
        regroup_unit(1)
        quantise_chunk(0, (0,))
        prepare_weights(2)
        prepare_weights(4)
        quantise_chunk(0, (1,))
        convolve(0)
        first_max(0)

        regroup_at = {0: [2], 1: [3], 2: [4], 3: [5]}
        spare, pairs = [], []
        difference_at = {4: (2, 0), 5: (2, 1), 6: (3, 0), 7: (3, 1)}
        for g in range(len(ROUNDS)):
            c, lead = ROUNDS[g]
            for u in regroup_at.get(g, ()):
                regroup_unit(u)
            if g == 5:
                regroup_unit(7)
                add_difference(2, 0)
            if g < 4:
                convolve(g + 1)
                first_max(g + 1)
            elif g < FINAL:
                convolve(g + 1, (0,), pairs[2 * (g - 4) % 3])
                first_max(g + 1)
                if g == 7:
                    store_q(2, turn_q(2, spare[0]))
                    convolve(g + 1, (1,), pairs[(2 * (g - 4) + 1) % 3])
                if g in difference_at:
                    convolve_difference(*difference_at[g], spare)
                    if g > 4:
                        add_difference(*difference_at[g])
                if g != 7:
                    convolve(g + 1, (1,), pairs[(2 * (g - 4) + 1) % 3])
            if g == 1:
                store_q(0, turn_q(0))
            if g == 3:
                regroup_unit(6)
            if g == FINAL:
                store_q(3, turn_q(3, spare[0]))
            rest_max(g)
            if g == 1:
                quantise_chunk(1)
            if g == 3:
                banks_in_turn = [(len(turn) - N_BANKS + i) % N_BANKS for i in range(N_BANKS)]
                spare = banks_in_turn[0:2]
                pairs = [banks_in_turn[i : i + 2] for i in (2, 4, 6)]
                store_q(1, turn_q(1, spare[0]))
                negate_weights()
                quantise_chunk(2, (0,))
                quantise_negative_weights()
                quantise_chunk(2, (1,))
            if g == 5:
                quantise_chunk(3)
            if g < FINAL:
                store_round(g)
